import numpy as np
import ml_dtypes


def mxq(x, axis, fmt="e4m3"):
    dtype, down = {"e4m3": (ml_dtypes.float8_e4m3fn, 7), "e5m2": (ml_dtypes.float8_e5m2, 14)}[fmt]
    v = np.moveaxis(np.asarray(x, np.float32).astype(ml_dtypes.bfloat16).astype(np.float64), axis, -1)
    blocks = v.reshape(v.shape[:-1] + (-1, 32))
    amax = np.abs(blocks).max(-1, keepdims=True)
    byte = np.maximum(np.where(amax > 0, np.frexp(amax)[1] - 1 + 127, 0) - down, 1)
    scale = np.exp2(byte - 127.0)
    codes = (blocks / scale).astype(np.float32).astype(dtype).astype(np.float64)
    return np.moveaxis((codes * scale).reshape(v.shape), -1, axis)


WIDE = False


def mx_kscale(k):
    if not WIDE:
        return np.ones(k)
    levels = np.array([10, -10, 5, -5, 0])
    a = np.random.permutation(np.resize(levels, k // 512 * 4)).reshape(k // 512, 4)
    idx = np.arange(k)
    return np.exp2(a[idx // 512, idx % 128 // 32])


BF16 = ml_dtypes.bfloat16


def bf(x):
    return np.asarray(x, np.float32).astype(BF16)


def f64(x):
    return np.asarray(x).astype(np.float64)


B, C, NP, P, HID = 128, 2, 8, 16, 256
IN_D = C * P * P
SEQ = NP * NP + 1
IMG = NP * P


def positional_embedding(seq_len, dim):
    i = np.arange(seq_len)[:, None].astype(np.float64)
    j = np.arange(dim)[None, :].astype(np.float64)
    ang = i / np.power(100000.0, j / dim)
    return np.where(j % 2 == 0, np.sin(ang), np.cos(ang))


def setup_inputs():
    s = mx_kscale(IN_D)
    X = np.random.standard_normal((B, C, NP, P, NP, P)) * s.reshape(1, C, 1, P, 1, P)
    bound = 2.0 / np.sqrt(IN_D)
    return {"X": bf(X.reshape(B, C, IMG, IMG)),
            "W": bf(np.random.uniform(-bound, bound, (HID, IN_D)) / s[None, :]),
            "b": bf(np.random.standard_normal(HID) * 0.3),
            "class_token": bf(np.random.uniform(0.0, 1.0, (1, HID))),
            "pos_embed": bf(positional_embedding(SEQ, HID))}


def reference(X, W, b, class_token, pos_embed):
    nb = X.shape[0]
    patches = f64(X).reshape(nb, C, NP, P, NP, P)
    patches = patches.transpose(0, 2, 4, 1, 3, 5).reshape(nb, NP * NP, IN_D)
    tokens = (mxq(patches, 2, "e4m3") @ mxq(f64(W), 1, "e4m3").T) + f64(b)
    cls = np.broadcast_to(f64(class_token)[None, :, :], (nb, 1, HID))
    tokens = np.concatenate([cls, tokens], axis=1)
    return tokens * f64(pos_embed)[None, :, :]

@@ -1,0 +1,140 @@
+from contextlib import ExitStack
+
+import concourse.mybir as mybir
+from concourse.masks import make_identity
+
+BF16 = mybir.dt.bfloat16
+F32 = mybir.dt.float32
+U32 = mybir.dt.uint32
+U8 = mybir.dt.uint8
+FP8X4 = mybir.dt.float8_e4m3fn_x4
+ADD = mybir.AluOpType.add
+MULT = mybir.AluOpType.mult
+
+FLOPS = 2 * 8192 * 512 * 256
+
+UNITS = 8
+G_COLS = 768
+
+
+def tile_myvit_t_kernel(tc, X, W, b, class_token, pos_embed, out):
+    nc = tc.nc
+    with ExitStack() as ctx:
+        const = ctx.enter_context(tc.tile_pool(name="const", bufs=1))
+        xin = ctx.enter_context(tc.tile_pool(name="xin", bufs=1))
+        work = ctx.enter_context(tc.tile_pool(name="work", bufs=3))
+        outp = ctx.enter_context(tc.tile_pool(name="outp", bufs=3))
+        psum = ctx.enter_context(tc.psum_pool(name="psum", bufs=4))
+
+        w_sb = const.tile([128, 2, 512], BF16, name="w_sb")
+        nc.scalar.dma_start(out=w_sb[:], in_=W.rearrange("(hh h) k -> h hh k", hh=2))
+        xrows = X.rearrange("n c (gy py) x -> (n c gy) (py x)", gy=8)
+        xs = []
+        for u in range(UNITS):
+            xt = xin.tile([128, 2, 2048], BF16, name="xs%d" % u)
+            for g in range(2):
+                r0 = (2 * u + g) * 128
+                nc.sync.dma_start(out=xt[:, g, :], in_=xrows[r0 : r0 + 128, :])
+            xs.append(xt)
+
+        z = const.tile([128, 768], BF16, name="z")
+        nc.vector.memset(z[:], 0.0)
+        nc.scalar.dma_start(out=z[0:1, 0:256], in_=b.unsqueeze(0))
+        nc.scalar.dma_start(out=z[0:1, 256:512], in_=class_token)
+        nc.scalar.dma_start(out=z[0:1, 512:768], in_=pos_embed[0:1, :])
+        pos_a = const.tile([128, 2048], BF16, name="pos_a")
+        pos_rows = pos_embed[1:65, :].rearrange("(gy gx) h -> gy (gx h)", gx=8)
+        nc.scalar.dma_start(
+            out=pos_a[:],
+            in_=pos_rows.unsqueeze(0).to_broadcast([16, 8, 2048]),
+        )
+
+        ident = const.tile([128, 128], F32, name="ident")
+        make_identity(nc, ident[:])
+        ones = const.tile([128, 128], BF16, name="ones")
+        nc.vector.memset(ones[:], 1.0)
+
+        wt = psum.tile([128, 4, 128], F32, name="wt", tag="tp")
+        w32 = w_sb[:].bitcast(F32)
+        for hh in range(2):
+            for c in range(2):
+                nc.tensor.transpose(wt[:, hh * 2 + c, :], w32[:, hh, c * 128 : (c + 1) * 128], ident[:])
+        wg = const.tile([128, 1024], BF16, name="wg", align_bytes=64)
+        nc.vector.tensor_copy(
+            out=wg[:].bitcast(F32).rearrange("p (hh h c) -> p hh h c", hh=2, c=2),
+            in_=wt[:].rearrange("p (hh c) h -> p hh h c", hh=2),
+        )
+        wcodes = const.tile([128, 256], U32, name="wcodes", align_bytes=64)
+        wscl = const.tile([128, 256], U8, name="wscl", align_bytes=64)
+        nc.vector.quantize_mx(out=wcodes[:].bitcast(FP8X4), scales=wscl[:], in_=wg[:])
+
+        zp0 = psum.tile([128, 512], F32, name="zp0", tag="acc")
+        nc.tensor.matmul(out=zp0[:], lhsT=ones[:], rhs=z[:, 0:512], start=True, stop=True)
+        zp1 = psum.tile([128, 256], F32, name="zp1", tag="acc")
+        nc.tensor.matmul(out=zp1[:], lhsT=ones[:], rhs=z[:, 512:768], start=True, stop=True)
+        bias_b = const.tile([128, 256], F32, name="bias_b")
+        nc.vector.tensor_copy(out=bias_b[:], in_=zp0[:, 0:256])
+        pos0 = const.tile([128, 256], F32, name="pos0")
+        nc.vector.tensor_copy(out=pos0[:], in_=zp1[:])
+        cls_sb = const.tile([128, 256], F32, name="cls_sb")
+        nc.vector.tensor_tensor(out=cls_sb[:], in0=zp0[:, 256:512], in1=pos0[:], op=MULT)
+        nc.sync.dma_start(out=out[:, 0, :], in_=cls_sb[:])
+
+        out_u = out[:, 1:65, :].rearrange("(u n) (gy gx) h -> u n gy (gx h)", n=16, gx=8)
+
+        for u in range(UNITS):
+            xp = work.tile([128, 2, 8, 128], F32, name="xp")
+            for g in range(2):
+                if u == 0:
+                    nc.vector.tensor_copy(
+                        out=xp[:, g].bitcast(BF16).rearrange("p gx (py px) -> p gx py px", px=16),
+                        in_=xs[u][:, g, :].rearrange("p (py gx px) -> p gx py px", py=16, gx=8),
+                    )
+                else:
+                    nc.scalar.copy(
+                        out=xp[:, g].rearrange("p gx (py w) -> p gx py w", w=8),
+                        in_=xs[u][:, g, :].bitcast(F32).rearrange("p (py gx w) -> p gx py w", py=16, gx=8),
+                    )
+            gq = work.tile([128, 4096], BF16, name="gq", align_bytes=64)
+            gq32 = gq[:].bitcast(F32)
+            for j in range(4):
+                tp = psum.tile([128, 4, 128], F32, name="tp", tag="tp")
+                for s in range(4):
+                    nc.tensor.transpose(tp[:, s, :], xp[:, s % 2, 2 * j + s // 2, :], ident[:])
+                dst = gq32[:, j * 512 : (j + 1) * 512].rearrange("p (a gy c) -> p a gy c", gy=8, c=2)
+                src = tp[:].rearrange("p s (nl c gy) -> p (s nl) gy c", nl=8, c=2)
+                if u == 0 and j % 2 == 1:
+                    nc.vector.tensor_copy(out=dst, in_=src)
+                else:
+                    nc.scalar.copy(out=dst, in_=src)
+            codes = work.tile([128, 1024], U32, name="codes", align_bytes=64)
+            scl = work.tile([128, 1024], U8, name="scl", align_bytes=64)
+            for q in range(2):
+                nc.vector.quantize_mx(
+                    out=codes[:, q * 512 : (q + 1) * 512].bitcast(FP8X4),
+                    scales=scl[:, q * 512 : (q + 1) * 512],
+                    in_=gq[:, q * 2048 : (q + 1) * 2048],
+                )
+            osb = outp.tile([128, 2048], F32, name="osb")
+            for j in range(4):
+                acc = psum.tile([128, 2, 256], F32, name="acc", tag="acc")
+                for s in range(2):
+                    gx = 2 * j + s
+                    nc.tensor.matmul_mx(
+                        out=acc[:, s, :],
+                        lhsT=codes[:, gx * 128 : (gx + 1) * 128].bitcast(FP8X4),
+                        lhsT_scale=scl[:, gx * 128 : (gx + 1) * 128],
+                        rhs=wcodes[:].bitcast(FP8X4),
+                        rhs_scale=wscl[:],
+                        start=True,
+                        stop=True,
+                    )
+                nc.vector.tensor_tensor(
+                    out=osb[:, j * 512 : (j + 1) * 512].rearrange("p (s h) -> p s h", s=2),
+                    in0=acc[:],
+                    in1=bias_b[:].unsqueeze(1).to_broadcast([128, 2, 256]),
+                    op=ADD,
+                )
+            nc.gpsimd.tensor_tensor(out=osb[:, 0:G_COLS], in0=osb[:, 0:G_COLS], in1=pos_a[:, 0:G_COLS], op=MULT)
+            nc.vector.tensor_tensor(out=osb[:, G_COLS:2048], in0=osb[:, G_COLS:2048], in1=pos_a[:, G_COLS:2048], op=MULT)
+            nc.sync.dma_start(out=out_u[u], in_=osb[:])

@@ -14,7 +14,7 @@ MULT = mybir.AluOpType.mult
 FLOPS = 2 * 8192 * 512 * 256
 
 UNITS = 8
-G_COLS = 768
+G_COLS = 0
 
 
 def tile_myvit_t_kernel(tc, X, W, b, class_token, pos_embed, out):
@@ -30,24 +30,29 @@ def tile_myvit_t_kernel(tc, X, W, b, class_token, pos_embed, out):
         nc.scalar.dma_start(out=w_sb[:], in_=W.rearrange("(hh h) k -> h hh k", hh=2))
         xrows = X.rearrange("n c (gy py) x -> (n c gy) (py x)", gy=8)
         xs = []
-        for u in range(UNITS):
+
+        def load_unit(u):
             xt = xin.tile([128, 2, 2048], BF16, name="xs%d" % u)
             for g in range(2):
                 r0 = (2 * u + g) * 128
                 nc.sync.dma_start(out=xt[:, g, :], in_=xrows[r0 : r0 + 128, :])
             xs.append(xt)
 
+        load_unit(0)
         z = const.tile([128, 768], BF16, name="z")
         nc.vector.memset(z[:], 0.0)
         nc.scalar.dma_start(out=z[0:1, 0:256], in_=b.unsqueeze(0))
         nc.scalar.dma_start(out=z[0:1, 256:512], in_=class_token)
         nc.scalar.dma_start(out=z[0:1, 512:768], in_=pos_embed[0:1, :])
+        load_unit(1)
         pos_a = const.tile([128, 2048], BF16, name="pos_a")
         pos_rows = pos_embed[1:65, :].rearrange("(gy gx) h -> gy (gx h)", gx=8)
         nc.scalar.dma_start(
             out=pos_a[:],
             in_=pos_rows.unsqueeze(0).to_broadcast([16, 8, 2048]),
         )
+        for u in range(2, UNITS):
+            load_unit(u)
 
         ident = const.tile([128, 128], F32, name="ident")
         make_identity(nc, ident[:])
@@ -135,6 +140,7 @@ def tile_myvit_t_kernel(tc, X, W, b, class_token, pos_embed, out):
                     in1=bias_b[:].unsqueeze(1).to_broadcast([128, 2, 256]),
                     op=ADD,
                 )
-            nc.gpsimd.tensor_tensor(out=osb[:, 0:G_COLS], in0=osb[:, 0:G_COLS], in1=pos_a[:, 0:G_COLS], op=MULT)
+            if G_COLS > 0:
+                nc.gpsimd.tensor_tensor(out=osb[:, 0:G_COLS], in0=osb[:, 0:G_COLS], in1=pos_a[:, 0:G_COLS], op=MULT)
             nc.vector.tensor_tensor(out=osb[:, G_COLS:2048], in0=osb[:, G_COLS:2048], in1=pos_a[:, G_COLS:2048], op=MULT)
             nc.sync.dma_start(out=out_u[u], in_=osb[:])

@@ -8,13 +8,13 @@ F32 = mybir.dt.float32
 U32 = mybir.dt.uint32
 U8 = mybir.dt.uint8
 FP8X4 = mybir.dt.float8_e4m3fn_x4
-ADD = mybir.AluOpType.add
 MULT = mybir.AluOpType.mult
+IDENT = mybir.ActivationFunctionType.Identity
 
 FLOPS = 2 * 8192 * 512 * 256
 
 UNITS = 8
-G_COLS = 0
+ITEMS = 16
 
 
 def tile_myvit_t_kernel(tc, X, W, b, class_token, pos_embed, out):
@@ -24,7 +24,17 @@ def tile_myvit_t_kernel(tc, X, W, b, class_token, pos_embed, out):
         xin = ctx.enter_context(tc.tile_pool(name="xin", bufs=1))
         work = ctx.enter_context(tc.tile_pool(name="work", bufs=3))
         outp = ctx.enter_context(tc.tile_pool(name="outp", bufs=3))
-        psum = ctx.enter_context(tc.psum_pool(name="psum", bufs=4))
+        ps_tp = ctx.enter_context(tc.psum_pool(name="ps_tp", bufs=3))
+        ps_mid = ctx.enter_context(tc.psum_pool(name="ps_mid", bufs=2))
+        ps_fin = ctx.enter_context(tc.psum_pool(name="ps_fin", bufs=3))
+        ctx.enter_context(tc.manual_schedule())
+
+        z = const.tile([128, 768], BF16, name="z")
+        nc.vector.memset(z[:], 0.0)
+        ones = const.tile([128, 128], BF16, name="ones")
+        nc.vector.memset(ones[:], 1.0)
+        ident = const.tile([128, 128], F32, name="ident")
+        make_identity(nc, ident[:])
 
         w_sb = const.tile([128, 2, 512], BF16, name="w_sb")
         nc.scalar.dma_start(out=w_sb[:], in_=W.rearrange("(hh h) k -> h hh k", hh=2))
@@ -39,27 +49,17 @@ def tile_myvit_t_kernel(tc, X, W, b, class_token, pos_embed, out):
             xs.append(xt)
 
         load_unit(0)
-        z = const.tile([128, 768], BF16, name="z")
-        nc.vector.memset(z[:], 0.0)
         nc.scalar.dma_start(out=z[0:1, 0:256], in_=b.unsqueeze(0))
         nc.scalar.dma_start(out=z[0:1, 256:512], in_=class_token)
         nc.scalar.dma_start(out=z[0:1, 512:768], in_=pos_embed[0:1, :])
         load_unit(1)
         pos_a = const.tile([128, 2048], BF16, name="pos_a")
         pos_rows = pos_embed[1:65, :].rearrange("(gy gx) h -> gy (gx h)", gx=8)
-        nc.scalar.dma_start(
-            out=pos_a[:],
-            in_=pos_rows.unsqueeze(0).to_broadcast([16, 8, 2048]),
-        )
+        nc.scalar.dma_start(out=pos_a[:], in_=pos_rows.unsqueeze(0).to_broadcast([16, 8, 2048]))
         for u in range(2, UNITS):
             load_unit(u)
 
-        ident = const.tile([128, 128], F32, name="ident")
-        make_identity(nc, ident[:])
-        ones = const.tile([128, 128], BF16, name="ones")
-        nc.vector.memset(ones[:], 1.0)
-
-        wt = psum.tile([128, 4, 128], F32, name="wt", tag="tp")
+        wt = ps_tp.tile([128, 4, 128], F32, name="wt", tag="tp")
         w32 = w_sb[:].bitcast(F32)
         for hh in range(2):
             for c in range(2):
@@ -73,74 +73,130 @@ def tile_myvit_t_kernel(tc, X, W, b, class_token, pos_embed, out):
         wscl = const.tile([128, 256], U8, name="wscl", align_bytes=64)
         nc.vector.quantize_mx(out=wcodes[:].bitcast(FP8X4), scales=wscl[:], in_=wg[:])
 
-        zp0 = psum.tile([128, 512], F32, name="zp0", tag="acc")
-        nc.tensor.matmul(out=zp0[:], lhsT=ones[:], rhs=z[:, 0:512], start=True, stop=True)
-        zp1 = psum.tile([128, 256], F32, name="zp1", tag="acc")
-        nc.tensor.matmul(out=zp1[:], lhsT=ones[:], rhs=z[:, 512:768], start=True, stop=True)
-        bias_b = const.tile([128, 256], F32, name="bias_b")
-        nc.vector.tensor_copy(out=bias_b[:], in_=zp0[:, 0:256])
-        pos0 = const.tile([128, 256], F32, name="pos0")
-        nc.vector.tensor_copy(out=pos0[:], in_=zp1[:])
-        cls_sb = const.tile([128, 256], F32, name="cls_sb")
-        nc.vector.tensor_tensor(out=cls_sb[:], in0=zp0[:, 256:512], in1=pos0[:], op=MULT)
-        nc.sync.dma_start(out=out[:, 0, :], in_=cls_sb[:])
-
         out_u = out[:, 1:65, :].rearrange("(u n) (gy gx) h -> u n gy (gx h)", n=16, gx=8)
+        b_col = const.tile([128, 2], F32, name="b_col")
 
-        for u in range(UNITS):
-            xp = work.tile([128, 2, 8, 128], F32, name="xp")
-            for g in range(2):
-                if u == 0:
-                    nc.vector.tensor_copy(
-                        out=xp[:, g].bitcast(BF16).rearrange("p gx (py px) -> p gx py px", px=16),
-                        in_=xs[u][:, g, :].rearrange("p (py gx px) -> p gx py px", py=16, gx=8),
-                    )
-                else:
-                    nc.scalar.copy(
-                        out=xp[:, g].rearrange("p gx (py w) -> p gx py w", w=8),
-                        in_=xs[u][:, g, :].bitcast(F32).rearrange("p (py gx w) -> p gx py w", py=16, gx=8),
-                    )
-            gq = work.tile([128, 4096], BF16, name="gq", align_bytes=64)
-            gq32 = gq[:].bitcast(F32)
-            for j in range(4):
-                tp = psum.tile([128, 4, 128], F32, name="tp", tag="tp")
+        def small_stuff():
+            bc = ps_mid.tile([128, 2, 64], F32, name="bc", tag="mid")
+            for hh in range(2):
+                nc.tensor.matmul(out=bc[:, hh, :], lhsT=z[:, hh * 128 : (hh + 1) * 128], rhs=ones[:, 0:64], start=True, stop=True)
+            nc.vector.tensor_copy(out=b_col[:], in_=bc[:, :, 0])
+            zp = ps_fin.tile([128, 512], F32, name="zp", tag="fin")
+            nc.tensor.matmul(out=zp[:], lhsT=ones[:], rhs=z[:, 256:768], start=True, stop=True)
+            pos0 = const.tile([128, 256], F32, name="pos0")
+            nc.vector.tensor_copy(out=pos0[:], in_=zp[:, 256:512])
+            cls_sb = const.tile([128, 256], F32, name="cls_sb")
+            nc.vector.tensor_tensor(out=cls_sb[:], in0=zp[:, 0:256], in1=pos0[:], op=MULT)
+            nc.sync.dma_start(out=out[:, 0, :], in_=cls_sb[:])
+
+        st = {}
+
+        def regroup(i):
+            u, hf = i // 2, i % 2
+            xp = work.tile([128, 2, 4, 128], F32, name="xp")
+            src = xs[u][:].rearrange("p g (py gx px) -> p g gx py px", py=16, gx=8)
+            nc.vector.tensor_copy(
+                out=xp[:].bitcast(BF16).rearrange("p g gx (py px) -> p g gx py px", px=16),
+                in_=src[:, :, hf * 4 : (hf + 1) * 4],
+            )
+            st[("xp", i)] = xp
+
+        def t_in(i):
+            xp = st[("xp", i)]
+            for jb in range(2):
+                tp = ps_tp.tile([128, 4, 128], F32, name="tp", tag="tp")
                 for s in range(4):
-                    nc.tensor.transpose(tp[:, s, :], xp[:, s % 2, 2 * j + s // 2, :], ident[:])
-                dst = gq32[:, j * 512 : (j + 1) * 512].rearrange("p (a gy c) -> p a gy c", gy=8, c=2)
-                src = tp[:].rearrange("p s (nl c gy) -> p (s nl) gy c", nl=8, c=2)
-                if u == 0 and j % 2 == 1:
-                    nc.vector.tensor_copy(out=dst, in_=src)
-                else:
-                    nc.scalar.copy(out=dst, in_=src)
-            codes = work.tile([128, 1024], U32, name="codes", align_bytes=64)
-            scl = work.tile([128, 1024], U8, name="scl", align_bytes=64)
-            for q in range(2):
-                nc.vector.quantize_mx(
-                    out=codes[:, q * 512 : (q + 1) * 512].bitcast(FP8X4),
-                    scales=scl[:, q * 512 : (q + 1) * 512],
-                    in_=gq[:, q * 2048 : (q + 1) * 2048],
+                    nc.tensor.transpose(tp[:, s, :], xp[:, s % 2, 2 * jb + s // 2, :], ident[:])
+                st[("tp", i, jb)] = tp
+
+        def e_in(i):
+            gq = work.tile([128, 2048], BF16, name="gq", align_bytes=64)
+            gq32 = gq[:].bitcast(F32)
+            for jb in range(2):
+                nc.scalar.copy(
+                    out=gq32[:, jb * 512 : (jb + 1) * 512].rearrange("p (a gy c) -> p a gy c", gy=8, c=2),
+                    in_=st[("tp", i, jb)][:].rearrange("p s (nl c gy) -> p (s nl) gy c", nl=8, c=2),
                 )
-            osb = outp.tile([128, 2048], F32, name="osb")
-            for j in range(4):
-                acc = psum.tile([128, 2, 256], F32, name="acc", tag="acc")
-                for s in range(2):
-                    gx = 2 * j + s
-                    nc.tensor.matmul_mx(
-                        out=acc[:, s, :],
-                        lhsT=codes[:, gx * 128 : (gx + 1) * 128].bitcast(FP8X4),
-                        lhsT_scale=scl[:, gx * 128 : (gx + 1) * 128],
-                        rhs=wcodes[:].bitcast(FP8X4),
-                        rhs_scale=wscl[:],
-                        start=True,
-                        stop=True,
-                    )
-                nc.vector.tensor_tensor(
-                    out=osb[:, j * 512 : (j + 1) * 512].rearrange("p (s h) -> p s h", s=2),
-                    in0=acc[:],
-                    in1=bias_b[:].unsqueeze(1).to_broadcast([128, 2, 256]),
-                    op=ADD,
+            st[("gq", i)] = gq
+
+        def quant(i):
+            codes = work.tile([128, 512], U32, name="codes", align_bytes=64)
+            scl = work.tile([128, 512], U8, name="scl", align_bytes=64)
+            nc.vector.quantize_mx(out=codes[:].bitcast(FP8X4), scales=scl[:], in_=st[("gq", i)][:])
+            st[("codes", i)] = codes
+            st[("scl", i)] = scl
+
+        def mx(i):
+            for hh in range(2):
+                mid = ps_mid.tile([128, 512], F32, name="mid", tag="mid")
+                nc.tensor.matmul_mx(
+                    out=mid[:],
+                    lhsT=wcodes[:, hh * 128 : (hh + 1) * 128].bitcast(FP8X4),
+                    lhsT_scale=wscl[:, hh * 128 : (hh + 1) * 128],
+                    rhs=st[("codes", i)][:].bitcast(FP8X4),
+                    rhs_scale=st[("scl", i)][:],
+                    start=True,
+                    stop=True,
                 )
-            if G_COLS > 0:
-                nc.gpsimd.tensor_tensor(out=osb[:, 0:G_COLS], in0=osb[:, 0:G_COLS], in1=pos_a[:, 0:G_COLS], op=MULT)
-            nc.vector.tensor_tensor(out=osb[:, G_COLS:2048], in0=osb[:, G_COLS:2048], in1=pos_a[:, G_COLS:2048], op=MULT)
-            nc.sync.dma_start(out=out_u[u], in_=osb[:])
+                st[("mid", i, hh)] = mid
+
+        def add_bias(i):
+            a_sb = work.tile([128, 2, 512], F32, name="a_sb")
+            for hh in range(2):
+                nc.scalar.activation(out=a_sb[:, hh, :], in_=st[("mid", i, hh)][:], func=IDENT, bias=b_col[:, hh : hh + 1], scale=1.0)
+            st[("a", i)] = a_sb
+
+        def t_out(i):
+            a_sb = st[("a", i)]
+            for jb in range(2):
+                fin = ps_fin.tile([128, 2, 256], F32, name="fin", tag="fin")
+                for gl in range(2):
+                    for hh in range(2):
+                        gx = 2 * jb + gl
+                        nc.tensor.transpose(fin[:, gl, hh * 128 : (hh + 1) * 128], a_sb[:, hh, gx * 128 : (gx + 1) * 128], ident[:])
+                st[("fin", i, jb)] = fin
+
+        def times_pos(i, jb):
+            u, hf = i // 2, i % 2
+            if hf == 0 and jb == 0:
+                st[("osb", u)] = outp.tile([128, 2048], F32, name="osb")
+            osb = st[("osb", u)]
+            c0 = hf * 1024 + jb * 512
+            nc.vector.tensor_tensor(
+                out=osb[:, c0 : c0 + 512].rearrange("p (s h) -> p s h", s=2),
+                in0=st[("fin", i, jb)][:],
+                in1=pos_a[:, c0 : c0 + 512].rearrange("p (s h) -> p s h", s=2),
+                op=MULT,
+            )
+
+        def store(i):
+            u, hf = i // 2, i % 2
+            if u == UNITS - 1:
+                nc.sync.dma_start(out=out_u[u][:, :, hf * 1024 : (hf + 1) * 1024], in_=st[("osb", u)][:, hf * 1024 : (hf + 1) * 1024])
+            elif hf == 1:
+                nc.sync.dma_start(out=out_u[u], in_=st[("osb", u)][:])
+
+        def on(i):
+            return 0 <= i < ITEMS
+
+        for k in range(-1, ITEMS + 2):
+            if on(k - 2):
+                t_out(k - 2)
+            if on(k):
+                e_in(k)
+            if on(k + 1):
+                regroup(k + 1)
+            if k == 0:
+                small_stuff()
+            if on(k - 2):
+                times_pos(k - 2, 0)
+            if on(k - 1):
+                mx(k - 1)
+                add_bias(k - 1)
+            if on(k):
+                quant(k)
+            if on(k + 1):
+                t_in(k + 1)
+            if on(k - 2):
+                times_pos(k - 2, 1)
+                store(k - 2)

@@ -22,7 +22,7 @@ def tile_myvit_t_kernel(tc, X, W, b, class_token, pos_embed, out):
     with ExitStack() as ctx:
         const = ctx.enter_context(tc.tile_pool(name="const", bufs=1))
         xin = ctx.enter_context(tc.tile_pool(name="xin", bufs=1))
-        work = ctx.enter_context(tc.tile_pool(name="work", bufs=3))
+        work = ctx.enter_context(tc.tile_pool(name="work", bufs=4))
         outp = ctx.enter_context(tc.tile_pool(name="outp", bufs=3))
         ps_tp = ctx.enter_context(tc.psum_pool(name="ps_tp", bufs=3))
         ps_mid = ctx.enter_context(tc.psum_pool(name="ps_mid", bufs=2))
@@ -101,23 +101,21 @@ def tile_myvit_t_kernel(tc, X, W, b, class_token, pos_embed, out):
             )
             st[("xp", i)] = xp
 
-        def t_in(i):
+        def t_in(i, jb):
             xp = st[("xp", i)]
-            for jb in range(2):
-                tp = ps_tp.tile([128, 4, 128], F32, name="tp", tag="tp")
-                for s in range(4):
-                    nc.tensor.transpose(tp[:, s, :], xp[:, s % 2, 2 * jb + s // 2, :], ident[:])
-                st[("tp", i, jb)] = tp
+            tp = ps_tp.tile([128, 4, 128], F32, name="tp", tag="tp")
+            for s in range(4):
+                nc.tensor.transpose(tp[:, s, :], xp[:, s % 2, 2 * jb + s // 2, :], ident[:])
+            st[("tp", i, jb)] = tp
 
-        def e_in(i):
-            gq = work.tile([128, 2048], BF16, name="gq", align_bytes=64)
-            gq32 = gq[:].bitcast(F32)
-            for jb in range(2):
-                nc.scalar.copy(
-                    out=gq32[:, jb * 512 : (jb + 1) * 512].rearrange("p (a gy c) -> p a gy c", gy=8, c=2),
-                    in_=st[("tp", i, jb)][:].rearrange("p s (nl c gy) -> p (s nl) gy c", nl=8, c=2),
-                )
-            st[("gq", i)] = gq
+        def e_in(i, jb):
+            if jb == 0:
+                st[("gq", i)] = work.tile([128, 2048], BF16, name="gq", align_bytes=64)
+            gq32 = st[("gq", i)][:].bitcast(F32)
+            nc.scalar.copy(
+                out=gq32[:, jb * 512 : (jb + 1) * 512].rearrange("p (a gy c) -> p a gy c", gy=8, c=2),
+                in_=st[("tp", i, jb)][:].rearrange("p s (nl c gy) -> p (s nl) gy c", nl=8, c=2),
+            )
 
         def quant(i):
             codes = work.tile([128, 512], U32, name="codes", align_bytes=64)
@@ -126,35 +124,32 @@ def tile_myvit_t_kernel(tc, X, W, b, class_token, pos_embed, out):
             st[("codes", i)] = codes
             st[("scl", i)] = scl
 
-        def mx(i):
-            for hh in range(2):
-                mid = ps_mid.tile([128, 512], F32, name="mid", tag="mid")
-                nc.tensor.matmul_mx(
-                    out=mid[:],
-                    lhsT=wcodes[:, hh * 128 : (hh + 1) * 128].bitcast(FP8X4),
-                    lhsT_scale=wscl[:, hh * 128 : (hh + 1) * 128],
-                    rhs=st[("codes", i)][:].bitcast(FP8X4),
-                    rhs_scale=st[("scl", i)][:],
-                    start=True,
-                    stop=True,
-                )
-                st[("mid", i, hh)] = mid
+        def mx(i, hh):
+            mid = ps_mid.tile([128, 512], F32, name="mid", tag="mid")
+            nc.tensor.matmul_mx(
+                out=mid[:],
+                lhsT=wcodes[:, hh * 128 : (hh + 1) * 128].bitcast(FP8X4),
+                lhsT_scale=wscl[:, hh * 128 : (hh + 1) * 128],
+                rhs=st[("codes", i)][:].bitcast(FP8X4),
+                rhs_scale=st[("scl", i)][:],
+                start=True,
+                stop=True,
+            )
+            st[("mid", i, hh)] = mid
 
-        def add_bias(i):
-            a_sb = work.tile([128, 2, 512], F32, name="a_sb")
-            for hh in range(2):
-                nc.scalar.activation(out=a_sb[:, hh, :], in_=st[("mid", i, hh)][:], func=IDENT, bias=b_col[:, hh : hh + 1], scale=1.0)
-            st[("a", i)] = a_sb
+        def add_bias(i, hh):
+            if hh == 0:
+                st[("a", i)] = work.tile([128, 2, 512], F32, name="a_sb")
+            nc.scalar.activation(out=st[("a", i)][:, hh, :], in_=st[("mid", i, hh)][:], func=IDENT, bias=b_col[:, hh : hh + 1], scale=1.0)
 
-        def t_out(i):
+        def t_out(i, jb):
             a_sb = st[("a", i)]
-            for jb in range(2):
-                fin = ps_fin.tile([128, 2, 256], F32, name="fin", tag="fin")
-                for gl in range(2):
-                    for hh in range(2):
-                        gx = 2 * jb + gl
-                        nc.tensor.transpose(fin[:, gl, hh * 128 : (hh + 1) * 128], a_sb[:, hh, gx * 128 : (gx + 1) * 128], ident[:])
-                st[("fin", i, jb)] = fin
+            fin = ps_fin.tile([128, 2, 256], F32, name="fin", tag="fin")
+            for gl in range(2):
+                for hh in range(2):
+                    gx = 2 * jb + gl
+                    nc.tensor.transpose(fin[:, gl, hh * 128 : (hh + 1) * 128], a_sb[:, hh, gx * 128 : (gx + 1) * 128], ident[:])
+            st[("fin", i, jb)] = fin
 
         def times_pos(i, jb):
             u, hf = i // 2, i % 2
@@ -168,35 +163,45 @@ def tile_myvit_t_kernel(tc, X, W, b, class_token, pos_embed, out):
                 in1=pos_a[:, c0 : c0 + 512].rearrange("p (s h) -> p s h", s=2),
                 op=MULT,
             )
-
-        def store(i):
-            u, hf = i // 2, i % 2
-            if u == UNITS - 1:
-                nc.sync.dma_start(out=out_u[u][:, :, hf * 1024 : (hf + 1) * 1024], in_=st[("osb", u)][:, hf * 1024 : (hf + 1) * 1024])
-            elif hf == 1:
-                nc.sync.dma_start(out=out_u[u], in_=st[("osb", u)][:])
+            if i == ITEMS - 1:
+                nc.sync.dma_start(out=out_u[u][:, :, c0 : c0 + 512], in_=osb[:, c0 : c0 + 512])
+            elif i == ITEMS - 2:
+                if jb == 1:
+                    nc.sync.dma_start(out=out_u[u][:, :, 0:1024], in_=osb[:, 0:1024])
+            elif hf == 1 and jb == 1:
+                nc.sync.dma_start(out=out_u[u], in_=osb[:])
 
         def on(i):
             return 0 <= i < ITEMS
 
-        for k in range(-1, ITEMS + 2):
-            if on(k - 2):
-                t_out(k - 2)
-            if on(k):
-                e_in(k)
+        for k in range(-2, ITEMS + 2):
             if on(k + 1):
-                regroup(k + 1)
-            if k == 0:
+                t_in(k + 1, 0)
+            if on(k - 1):
+                add_bias(k - 1, 1)
+            if on(k - 2):
+                t_out(k - 2, 0)
+            if on(k + 2):
+                regroup(k + 2)
+            if k == -1:
                 small_stuff()
+            if on(k + 1):
+                t_in(k + 1, 1)
+            if on(k - 2):
+                t_out(k - 2, 1)
+            if on(k + 1):
+                e_in(k + 1, 0)
+            if on(k):
+                mx(k, 0)
             if on(k - 2):
                 times_pos(k - 2, 0)
-            if on(k - 1):
-                mx(k - 1)
-                add_bias(k - 1)
             if on(k):
-                quant(k)
+                mx(k, 1)
             if on(k + 1):
-                t_in(k + 1)
+                e_in(k + 1, 1)
             if on(k - 2):
                 times_pos(k - 2, 1)
-                store(k - 2)
+            if on(k):
+                add_bias(k, 0)
+            if on(k + 1):
+                quant(k + 1)

@@ -55,7 +55,7 @@ def tile_myvit_t_kernel(tc, X, W, b, class_token, pos_embed, out):
         load_unit(1)
         pos_a = const.tile([128, 2048], BF16, name="pos_a")
         pos_rows = pos_embed[1:65, :].rearrange("(gy gx) h -> gy (gx h)", gx=8)
-        nc.scalar.dma_start(out=pos_a[:], in_=pos_rows.unsqueeze(0).to_broadcast([16, 8, 2048]))
+        nc.sync.dma_start(out=pos_a[:], in_=pos_rows.unsqueeze(0).to_broadcast([16, 8, 2048]))
         for u in range(2, UNITS):
             load_unit(u)
 
@@ -65,13 +65,15 @@ def tile_myvit_t_kernel(tc, X, W, b, class_token, pos_embed, out):
             for c in range(2):
                 nc.tensor.transpose(wt[:, hh * 2 + c, :], w32[:, hh, c * 128 : (c + 1) * 128], ident[:])
         wg = const.tile([128, 1024], BF16, name="wg", align_bytes=64)
-        nc.vector.tensor_copy(
-            out=wg[:].bitcast(F32).rearrange("p (hh h c) -> p hh h c", hh=2, c=2),
-            in_=wt[:].rearrange("p (hh c) h -> p hh h c", hh=2),
-        )
         wcodes = const.tile([128, 256], U32, name="wcodes", align_bytes=64)
         wscl = const.tile([128, 256], U8, name="wscl", align_bytes=64)
-        nc.vector.quantize_mx(out=wcodes[:].bitcast(FP8X4), scales=wscl[:], in_=wg[:])
+
+        def quantise_w():
+            nc.vector.tensor_copy(
+                out=wg[:].bitcast(F32).rearrange("p (hh h c) -> p hh h c", hh=2, c=2),
+                in_=wt[:].rearrange("p (hh c) h -> p hh h c", hh=2),
+            )
+            nc.vector.quantize_mx(out=wcodes[:].bitcast(FP8X4), scales=wscl[:], in_=wg[:])
 
         out_u = out[:, 1:65, :].rearrange("(u n) (gy gx) h -> u n gy (gx h)", n=16, gx=8)
         b_col = const.tile([128, 2], F32, name="b_col")
@@ -100,6 +102,17 @@ def tile_myvit_t_kernel(tc, X, W, b, class_token, pos_embed, out):
                 in_=src[:, :, hf * 4 : (hf + 1) * 4],
             )
             st[("xp", i)] = xp
+
+        def regroup_first_unit():
+            src = xs[0][:].rearrange("p g (py gx px) -> p g gx py px", py=16, gx=8)
+            for i in range(2):
+                st[("xp", i)] = work.tile([128, 2, 4, 128], F32, name="xp")
+            for g in range(2):
+                for i in range(2):
+                    nc.vector.tensor_copy(
+                        out=st[("xp", i)][:, g].bitcast(BF16).rearrange("p gx (py px) -> p gx py px", px=16),
+                        in_=src[:, g, i * 4 : (i + 1) * 4],
+                    )
 
         def t_in(i, jb):
             xp = st[("xp", i)]
@@ -181,10 +194,13 @@ def tile_myvit_t_kernel(tc, X, W, b, class_token, pos_embed, out):
                 add_bias(k - 1, 1)
             if on(k - 2):
                 t_out(k - 2, 0)
-            if on(k + 2):
-                regroup(k + 2)
-            if k == -1:
+            if k == -2:
+                regroup_first_unit()
+            elif k == -1:
+                quantise_w()
                 small_stuff()
+            elif on(k + 2):
+                regroup(k + 2)
             if on(k + 1):
                 t_in(k + 1, 1)
             if on(k - 2):

@@ -13,7 +13,6 @@ IDENT = mybir.ActivationFunctionType.Identity
 
 FLOPS = 2 * 8192 * 512 * 256
 
-UNITS = 8
 ITEMS = 16
 
 
@@ -23,7 +22,7 @@ def tile_myvit_t_kernel(tc, X, W, b, class_token, pos_embed, out):
         const = ctx.enter_context(tc.tile_pool(name="const", bufs=1))
         xin = ctx.enter_context(tc.tile_pool(name="xin", bufs=1))
         work = ctx.enter_context(tc.tile_pool(name="work", bufs=4))
-        outp = ctx.enter_context(tc.tile_pool(name="outp", bufs=3))
+        outp = ctx.enter_context(tc.tile_pool(name="outp", bufs=4))
         ps_tp = ctx.enter_context(tc.psum_pool(name="ps_tp", bufs=3))
         ps_mid = ctx.enter_context(tc.psum_pool(name="ps_mid", bufs=2))
         ps_fin = ctx.enter_context(tc.psum_pool(name="ps_fin", bufs=3))
@@ -41,23 +40,28 @@ def tile_myvit_t_kernel(tc, X, W, b, class_token, pos_embed, out):
         xrows = X.rearrange("n c (gy py) x -> (n c gy) (py x)", gy=8)
         xs = []
 
-        def load_unit(u):
-            xt = xin.tile([128, 2, 2048], BF16, name="xs%d" % u)
-            for g in range(2):
-                r0 = (2 * u + g) * 128
-                nc.sync.dma_start(out=xt[:, g, :], in_=xrows[r0 : r0 + 128, :])
+        def load_item(i):
+            xt = xin.tile([128, 2048], BF16, name="xs%d" % i)
+            nc.sync.dma_start(out=xt[:], in_=xrows[i * 128 : (i + 1) * 128, :])
             xs.append(xt)
 
-        load_unit(0)
+        load_item(0)
         nc.scalar.dma_start(out=z[0:1, 0:256], in_=b.unsqueeze(0))
         nc.scalar.dma_start(out=z[0:1, 256:512], in_=class_token)
         nc.scalar.dma_start(out=z[0:1, 512:768], in_=pos_embed[0:1, :])
-        load_unit(1)
-        pos_a = const.tile([128, 2048], BF16, name="pos_a")
-        pos_rows = pos_embed[1:65, :].rearrange("(gy gx) h -> gy (gx h)", gx=8)
-        nc.sync.dma_start(out=pos_a[:], in_=pos_rows.unsqueeze(0).to_broadcast([16, 8, 2048]))
-        for u in range(2, UNITS):
-            load_unit(u)
+        load_item(1)
+        load_item(2)
+        pos_a = const.tile([128, 1024], BF16, name="pos_a")
+        pos_rows = pos_embed[1:65, :].rearrange("(q j) h -> q (j h)", j=4)
+        nc.sync.dma_start(out=pos_a[:], in_=pos_rows.unsqueeze(1).to_broadcast([16, 8, 1024]))
+        for i in range(3, ITEMS):
+            load_item(i)
+
+        perm = const.tile([128, 128], F32, name="perm")
+        nc.vector.tensor_copy(
+            out=perm[:].rearrange("p (gy nc) -> p gy nc", gy=8),
+            in_=ident[:].rearrange("p (nc gy) -> p gy nc", gy=8),
+        )
 
         wt = ps_tp.tile([128, 4, 128], F32, name="wt", tag="tp")
         w32 = w_sb[:].bitcast(F32)
@@ -75,14 +79,16 @@ def tile_myvit_t_kernel(tc, X, W, b, class_token, pos_embed, out):
             )
             nc.vector.quantize_mx(out=wcodes[:].bitcast(FP8X4), scales=wscl[:], in_=wg[:])
 
-        out_u = out[:, 1:65, :].rearrange("(u n) (gy gx) h -> u n gy (gx h)", n=16, gx=8)
+        out_i = out[:, 1:65, :].rearrange("(i n) (q j) h -> i q n (j h)", n=8, j=4)
         b_col = const.tile([128, 2], F32, name="b_col")
 
-        def small_stuff():
+        def bias_column():
             bc = ps_mid.tile([128, 2, 64], F32, name="bc", tag="mid")
             for hh in range(2):
                 nc.tensor.matmul(out=bc[:, hh, :], lhsT=z[:, hh * 128 : (hh + 1) * 128], rhs=ones[:, 0:64], start=True, stop=True)
             nc.vector.tensor_copy(out=b_col[:], in_=bc[:, :, 0])
+
+        def class_rows():
             zp = ps_fin.tile([128, 512], F32, name="zp", tag="fin")
             nc.tensor.matmul(out=zp[:], lhsT=ones[:], rhs=z[:, 256:768], start=True, stop=True)
             pos0 = const.tile([128, 256], F32, name="pos0")
@@ -94,31 +100,19 @@ def tile_myvit_t_kernel(tc, X, W, b, class_token, pos_embed, out):
         st = {}
 
         def regroup(i):
-            u, hf = i // 2, i % 2
-            xp = work.tile([128, 2, 4, 128], F32, name="xp")
-            src = xs[u][:].rearrange("p g (py gx px) -> p g gx py px", py=16, gx=8)
+            xp = work.tile([128, 8, 128], F32, name="xp")
             nc.vector.tensor_copy(
-                out=xp[:].bitcast(BF16).rearrange("p g gx (py px) -> p g gx py px", px=16),
-                in_=src[:, :, hf * 4 : (hf + 1) * 4],
+                out=xp[:].bitcast(BF16).rearrange("p gx (py px) -> p gx py px", px=16),
+                in_=xs[i][:].rearrange("p (py gx px) -> p gx py px", py=16, gx=8),
             )
             st[("xp", i)] = xp
-
-        def regroup_first_unit():
-            src = xs[0][:].rearrange("p g (py gx px) -> p g gx py px", py=16, gx=8)
-            for i in range(2):
-                st[("xp", i)] = work.tile([128, 2, 4, 128], F32, name="xp")
-            for g in range(2):
-                for i in range(2):
-                    nc.vector.tensor_copy(
-                        out=st[("xp", i)][:, g].bitcast(BF16).rearrange("p gx (py px) -> p gx py px", px=16),
-                        in_=src[:, g, i * 4 : (i + 1) * 4],
-                    )
 
         def t_in(i, jb):
             xp = st[("xp", i)]
             tp = ps_tp.tile([128, 4, 128], F32, name="tp", tag="tp")
             for s in range(4):
-                nc.tensor.transpose(tp[:, s, :], xp[:, s % 2, 2 * jb + s // 2, :], ident[:])
+                gxl, jj = s // 2, s % 2
+                nc.tensor.transpose(tp[:, s, :], xp[:, 4 * gxl + 2 * jb + jj, :], perm[:])
             st[("tp", i, jb)] = tp
 
         def e_in(i, jb):
@@ -126,8 +120,8 @@ def tile_myvit_t_kernel(tc, X, W, b, class_token, pos_embed, out):
                 st[("gq", i)] = work.tile([128, 2048], BF16, name="gq", align_bytes=64)
             gq32 = st[("gq", i)][:].bitcast(F32)
             nc.scalar.copy(
-                out=gq32[:, jb * 512 : (jb + 1) * 512].rearrange("p (a gy c) -> p a gy c", gy=8, c=2),
-                in_=st[("tp", i, jb)][:].rearrange("p s (nl c gy) -> p (s nl) gy c", nl=8, c=2),
+                out=gq32[:, jb * 512 : (jb + 1) * 512].rearrange("p (a gxl nc) -> p a gxl nc", gxl=2, nc=16),
+                in_=st[("tp", i, jb)][:].rearrange("p (gxl jj) (gy nc) -> p (jj gy) gxl nc", gxl=2, nc=16),
             )
 
         def quant(i):
@@ -158,18 +152,17 @@ def tile_myvit_t_kernel(tc, X, W, b, class_token, pos_embed, out):
         def t_out(i, jb):
             a_sb = st[("a", i)]
             fin = ps_fin.tile([128, 2, 256], F32, name="fin", tag="fin")
-            for gl in range(2):
+            for jj in range(2):
                 for hh in range(2):
-                    gx = 2 * jb + gl
-                    nc.tensor.transpose(fin[:, gl, hh * 128 : (hh + 1) * 128], a_sb[:, hh, gx * 128 : (gx + 1) * 128], ident[:])
+                    j = 2 * jb + jj
+                    nc.tensor.transpose(fin[:, jj, hh * 128 : (hh + 1) * 128], a_sb[:, hh, j * 128 : (j + 1) * 128], ident[:])
             st[("fin", i, jb)] = fin
 
         def times_pos(i, jb):
-            u, hf = i // 2, i % 2
-            if hf == 0 and jb == 0:
-                st[("osb", u)] = outp.tile([128, 2048], F32, name="osb")
-            osb = st[("osb", u)]
-            c0 = hf * 1024 + jb * 512
+            if jb == 0:
+                st[("osb", i)] = outp.tile([128, 1024], F32, name="osb")
+            osb = st[("osb", i)]
+            c0 = jb * 512
             nc.vector.tensor_tensor(
                 out=osb[:, c0 : c0 + 512].rearrange("p (s h) -> p s h", s=2),
                 in0=st[("fin", i, jb)][:],
@@ -177,12 +170,9 @@ def tile_myvit_t_kernel(tc, X, W, b, class_token, pos_embed, out):
                 op=MULT,
             )
             if i == ITEMS - 1:
-                nc.sync.dma_start(out=out_u[u][:, :, c0 : c0 + 512], in_=osb[:, c0 : c0 + 512])
-            elif i == ITEMS - 2:
-                if jb == 1:
-                    nc.sync.dma_start(out=out_u[u][:, :, 0:1024], in_=osb[:, 0:1024])
-            elif hf == 1 and jb == 1:
-                nc.sync.dma_start(out=out_u[u], in_=osb[:])
+                nc.sync.dma_start(out=out_i[i][:, :, c0 : c0 + 512], in_=osb[:, c0 : c0 + 512])
+            elif jb == 1:
+                nc.sync.dma_start(out=out_i[i], in_=osb[:])
 
         def on(i):
             return 0 <= i < ITEMS
@@ -194,12 +184,9 @@ def tile_myvit_t_kernel(tc, X, W, b, class_token, pos_embed, out):
                 add_bias(k - 1, 1)
             if on(k - 2):
                 t_out(k - 2, 0)
-            if k == -2:
-                regroup_first_unit()
-            elif k == -1:
+            if k == -1:
                 quantise_w()
-                small_stuff()
-            elif on(k + 2):
+            if on(k + 2):
                 regroup(k + 2)
             if on(k + 1):
                 t_in(k + 1, 1)
@@ -221,3 +208,7 @@ def tile_myvit_t_kernel(tc, X, W, b, class_token, pos_embed, out):
                 add_bias(k, 0)
             if on(k + 1):
                 quant(k + 1)
+            if k == -1:
+                bias_column()
+            if k == 0:
+                class_rows()

@@ -22,14 +22,15 @@ def tile_myvit_t_kernel(tc, X, W, b, class_token, pos_embed, out):
         const = ctx.enter_context(tc.tile_pool(name="const", bufs=1))
         xin = ctx.enter_context(tc.tile_pool(name="xin", bufs=1))
         work = ctx.enter_context(tc.tile_pool(name="work", bufs=4))
-        outp = ctx.enter_context(tc.tile_pool(name="outp", bufs=4))
+        ahead = ctx.enter_context(tc.tile_pool(name="ahead", bufs=6))
+        outp = ctx.enter_context(tc.tile_pool(name="outp", bufs=ITEMS))
         ps_tp = ctx.enter_context(tc.psum_pool(name="ps_tp", bufs=3))
         ps_mid = ctx.enter_context(tc.psum_pool(name="ps_mid", bufs=2))
         ps_fin = ctx.enter_context(tc.psum_pool(name="ps_fin", bufs=3))
         ctx.enter_context(tc.manual_schedule())
 
-        z = const.tile([128, 768], BF16, name="z")
-        nc.vector.memset(z[:], 0.0)
+        zb = const.tile([128, 256], BF16, name="zb")
+        nc.vector.memset(zb[:], 0.0)
         ones = const.tile([128, 128], BF16, name="ones")
         nc.vector.memset(ones[:], 1.0)
         ident = const.tile([128, 128], F32, name="ident")
@@ -46,9 +47,7 @@ def tile_myvit_t_kernel(tc, X, W, b, class_token, pos_embed, out):
             xs.append(xt)
 
         load_item(0)
-        nc.scalar.dma_start(out=z[0:1, 0:256], in_=b.unsqueeze(0))
-        nc.scalar.dma_start(out=z[0:1, 256:512], in_=class_token)
-        nc.scalar.dma_start(out=z[0:1, 512:768], in_=pos_embed[0:1, :])
+        nc.scalar.dma_start(out=zb[0:1, :], in_=b.unsqueeze(0))
         load_item(1)
         load_item(2)
         pos_a = const.tile([128, 1024], BF16, name="pos_a")
@@ -63,48 +62,54 @@ def tile_myvit_t_kernel(tc, X, W, b, class_token, pos_embed, out):
             in_=ident[:].rearrange("p (nc gy) -> p gy nc", gy=8),
         )
 
-        wt = ps_tp.tile([128, 4, 128], F32, name="wt", tag="tp")
-        w32 = w_sb[:].bitcast(F32)
-        for hh in range(2):
-            for c in range(2):
-                nc.tensor.transpose(wt[:, hh * 2 + c, :], w32[:, hh, c * 128 : (c + 1) * 128], ident[:])
         wg = const.tile([128, 1024], BF16, name="wg", align_bytes=64)
         wcodes = const.tile([128, 256], U32, name="wcodes", align_bytes=64)
         wscl = const.tile([128, 256], U8, name="wscl", align_bytes=64)
 
-        def quantise_w():
-            nc.vector.tensor_copy(
+        wt = ps_fin.tile([128, 4, 128], F32, name="wt", tag="fin")
+
+        def transpose_w():
+            w32 = w_sb[:].bitcast(F32)
+            for hh in range(2):
+                for c in range(2):
+                    nc.tensor.transpose(wt[:, hh * 2 + c, :], w32[:, hh, c * 128 : (c + 1) * 128], ident[:])
+
+        def regroup_w():
+            nc.scalar.copy(
                 out=wg[:].bitcast(F32).rearrange("p (hh h c) -> p hh h c", hh=2, c=2),
                 in_=wt[:].rearrange("p (hh c) h -> p hh h c", hh=2),
             )
+
+        def quantise_w():
             nc.vector.quantize_mx(out=wcodes[:].bitcast(FP8X4), scales=wscl[:], in_=wg[:])
 
         out_i = out[:, 1:65, :].rearrange("(i n) (q j) h -> i q n (j h)", n=8, j=4)
         b_col = const.tile([128, 2], F32, name="b_col")
 
         def bias_column():
-            bc = ps_mid.tile([128, 2, 64], F32, name="bc", tag="mid")
+            bc = ps_fin.tile([128, 2, 64], F32, name="bc", tag="fin")
             for hh in range(2):
-                nc.tensor.matmul(out=bc[:, hh, :], lhsT=z[:, hh * 128 : (hh + 1) * 128], rhs=ones[:, 0:64], start=True, stop=True)
+                nc.tensor.matmul(out=bc[:, hh, :], lhsT=zb[:, hh * 128 : (hh + 1) * 128], rhs=ones[:, 0:64], start=True, stop=True)
             nc.vector.tensor_copy(out=b_col[:], in_=bc[:, :, 0])
 
         def class_rows():
-            zp = ps_fin.tile([128, 512], F32, name="zp", tag="fin")
-            nc.tensor.matmul(out=zp[:], lhsT=ones[:], rhs=z[:, 256:768], start=True, stop=True)
-            pos0 = const.tile([128, 256], F32, name="pos0")
-            nc.vector.tensor_copy(out=pos0[:], in_=zp[:, 256:512])
+            cls_in = const.tile([128, 2, 256], BF16, name="cls_in")
+            nc.sync.dma_start(out=cls_in[:, 0, :], in_=class_token[0, :].partition_broadcast(128))
+            nc.sync.dma_start(out=cls_in[:, 1, :], in_=pos_embed[0, :].partition_broadcast(128))
             cls_sb = const.tile([128, 256], F32, name="cls_sb")
-            nc.vector.tensor_tensor(out=cls_sb[:], in0=zp[:, 0:256], in1=pos0[:], op=MULT)
+            nc.gpsimd.tensor_tensor(out=cls_sb[:], in0=cls_in[:, 0, :], in1=cls_in[:, 1, :], op=MULT)
             nc.sync.dma_start(out=out[:, 0, :], in_=cls_sb[:])
 
         st = {}
 
         def regroup(i):
-            xp = work.tile([128, 8, 128], F32, name="xp")
-            nc.vector.tensor_copy(
-                out=xp[:].bitcast(BF16).rearrange("p gx (py px) -> p gx py px", px=16),
-                in_=xs[i][:].rearrange("p (py gx px) -> p gx py px", py=16, gx=8),
-            )
+            xp = ahead.tile([128, 8, 128], F32, name="xp")
+            dst = xp[:].bitcast(BF16).rearrange("p gx (py px) -> p gx py px", px=16)
+            src = xs[i][:].rearrange("p (py gx px) -> p gx py px", py=16, gx=8)
+            nv = 8 if i < 2 else 6
+            nc.vector.tensor_copy(out=dst[:, 0:nv], in_=src[:, 0:nv])
+            if nv < 8:
+                nc.gpsimd.tensor_scalar(out=dst[:, nv:8], in0=src[:, nv:8], scalar1=1.0, scalar2=0.0, op0=MULT, op1=mybir.AluOpType.add)
             st[("xp", i)] = xp
 
         def t_in(i, jb):
@@ -149,6 +154,13 @@ def tile_myvit_t_kernel(tc, X, W, b, class_token, pos_embed, out):
                 st[("a", i)] = work.tile([128, 2, 512], F32, name="a_sb")
             nc.scalar.activation(out=st[("a", i)][:, hh, :], in_=st[("mid", i, hh)][:], func=IDENT, bias=b_col[:, hh : hh + 1], scale=1.0)
 
+        def add_bias_columns(i, jb):
+            if jb == 0:
+                st[("a", i)] = work.tile([128, 2, 512], F32, name="a_sb")
+            cols = slice(jb * 256, (jb + 1) * 256)
+            for hh in range(2):
+                nc.scalar.activation(out=st[("a", i)][:, hh, cols], in_=st[("mid", i, hh)][:, cols], func=IDENT, bias=b_col[:, hh : hh + 1], scale=1.0)
+
         def t_out(i, jb):
             a_sb = st[("a", i)]
             fin = ps_fin.tile([128, 2, 256], F32, name="fin", tag="fin")
@@ -162,36 +174,45 @@ def tile_myvit_t_kernel(tc, X, W, b, class_token, pos_embed, out):
             if jb == 0:
                 st[("osb", i)] = outp.tile([128, 1024], F32, name="osb")
             osb = st[("osb", i)]
-            c0 = jb * 512
-            nc.vector.tensor_tensor(
-                out=osb[:, c0 : c0 + 512].rearrange("p (s h) -> p s h", s=2),
-                in0=st[("fin", i, jb)][:],
-                in1=pos_a[:, c0 : c0 + 512].rearrange("p (s h) -> p s h", s=2),
-                op=MULT,
-            )
-            if i == ITEMS - 1:
-                nc.sync.dma_start(out=out_i[i][:, :, c0 : c0 + 512], in_=osb[:, c0 : c0 + 512])
-            elif jb == 1:
+            pieces = 2 if (i, jb) == (ITEMS - 1, 1) else 1
+            for s in range(pieces):
+                slots = slice(s, s + 1) if pieces == 2 else slice(0, 2)
+                c0 = jb * 512 + s * 256
+                c1 = c0 + 512 // pieces
+                nc.vector.tensor_tensor(
+                    out=osb[:, c0:c1].rearrange("p (s h) -> p s h", h=256),
+                    in0=st[("fin", i, jb)][:, slots, :],
+                    in1=pos_a[:, c0:c1].rearrange("p (s h) -> p s h", h=256),
+                    op=MULT,
+                )
+                if i == ITEMS - 1:
+                    nc.sync.dma_start(out=out_i[i][:, :, c0:c1], in_=osb[:, c0:c1])
+            if i < ITEMS - 1 and jb == 1:
                 nc.sync.dma_start(out=out_i[i], in_=osb[:])
 
         def on(i):
             return 0 <= i < ITEMS
 
-        for k in range(-2, ITEMS + 2):
+        last = ITEMS - 1
+        regroup(0)
+        regroup(1)
+        for k in range(-1, ITEMS + 2):
             if on(k + 1):
                 t_in(k + 1, 0)
-            if on(k - 1):
+            if on(k - 1) and k - 1 < last:
                 add_bias(k - 1, 1)
+            if k - 1 == last:
+                add_bias_columns(last, 1)
             if on(k - 2):
                 t_out(k - 2, 0)
-            if k == -1:
-                quantise_w()
-            if on(k + 2):
-                regroup(k + 2)
+            if k >= 2 and on(k + 4):
+                regroup(k + 4)
             if on(k + 1):
                 t_in(k + 1, 1)
             if on(k - 2):
                 t_out(k - 2, 1)
+            if k == -1:
+                transpose_w()
             if on(k + 1):
                 e_in(k + 1, 0)
             if on(k):
@@ -204,11 +225,22 @@ def tile_myvit_t_kernel(tc, X, W, b, class_token, pos_embed, out):
                 e_in(k + 1, 1)
             if on(k - 2):
                 times_pos(k - 2, 1)
-            if on(k):
+            if k == 0:
+                bias_column()
+                regroup(3)
+            if on(k) and k < last:
                 add_bias(k, 0)
+            if k == last:
+                add_bias_columns(last, 0)
             if on(k + 1):
                 quant(k + 1)
             if k == -1:
-                bias_column()
+                regroup_w()
+                quantise_w()
+                regroup(2)
             if k == 0:
+                regroup(4)
+            if k == 2:
                 class_rows()
+            if k == 1:
+                regroup(5)

@@ -37,18 +37,21 @@ def tile_myvit_t_kernel(tc, X, W, b, class_token, pos_embed, out):
         make_identity(nc, ident[:])
 
         w_sb = const.tile([128, 2, 512], BF16, name="w_sb")
-        nc.scalar.dma_start(out=w_sb[:], in_=W.rearrange("(hh h) k -> h hh k", hh=2))
         xrows = X.rearrange("n c (gy py) x -> (n c gy) (py x)", gy=8)
         xs = []
 
         def load_item(i):
             xt = xin.tile([128, 2048], BF16, name="xs%d" % i)
-            nc.sync.dma_start(out=xt[:], in_=xrows[i * 128 : (i + 1) * 128, :])
+            pieces = 2 if i == 0 else 1
+            for r in range(pieces):
+                cols = slice(r * 2048 // pieces, (r + 1) * 2048 // pieces)
+                nc.sync.dma_start(out=xt[:, cols], in_=xrows[i * 128 : (i + 1) * 128, cols])
             xs.append(xt)
 
         load_item(0)
-        nc.scalar.dma_start(out=zb[0:1, :], in_=b.unsqueeze(0))
         load_item(1)
+        nc.sync.dma_start(out=w_sb[:], in_=W.rearrange("(hh h) k -> h hh k", hh=2))
+        nc.sync.dma_start(out=zb[0:1, :], in_=b.unsqueeze(0))
         load_item(2)
         pos_a = const.tile([128, 1024], BF16, name="pos_a")
         pos_rows = pos_embed[1:65, :].rearrange("(q j) h -> q (j h)", j=4)
@@ -75,7 +78,7 @@ def tile_myvit_t_kernel(tc, X, W, b, class_token, pos_embed, out):
                     nc.tensor.transpose(wt[:, hh * 2 + c, :], w32[:, hh, c * 128 : (c + 1) * 128], ident[:])
 
         def regroup_w():
-            nc.scalar.copy(
+            nc.vector.tensor_copy(
                 out=wg[:].bitcast(F32).rearrange("p (hh h c) -> p hh h c", hh=2, c=2),
                 in_=wt[:].rearrange("p (hh c) h -> p hh h c", hh=2),
             )
@@ -92,10 +95,11 @@ def tile_myvit_t_kernel(tc, X, W, b, class_token, pos_embed, out):
                 nc.tensor.matmul(out=bc[:, hh, :], lhsT=zb[:, hh * 128 : (hh + 1) * 128], rhs=ones[:, 0:64], start=True, stop=True)
             nc.vector.tensor_copy(out=b_col[:], in_=bc[:, :, 0])
 
+        cls_in = const.tile([128, 2, 256], BF16, name="cls_in")
+        nc.sync.dma_start(out=cls_in[:, 0, :], in_=class_token[0, :].partition_broadcast(128))
+        nc.sync.dma_start(out=cls_in[:, 1, :], in_=pos_embed[0, :].partition_broadcast(128))
+
         def class_rows():
-            cls_in = const.tile([128, 2, 256], BF16, name="cls_in")
-            nc.sync.dma_start(out=cls_in[:, 0, :], in_=class_token[0, :].partition_broadcast(128))
-            nc.sync.dma_start(out=cls_in[:, 1, :], in_=pos_embed[0, :].partition_broadcast(128))
             cls_sb = const.tile([128, 256], F32, name="cls_sb")
             nc.gpsimd.tensor_tensor(out=cls_sb[:], in0=cls_in[:, 0, :], in1=cls_in[:, 1, :], op=MULT)
             nc.sync.dma_start(out=out[:, 0, :], in_=cls_sb[:])
@@ -106,10 +110,10 @@ def tile_myvit_t_kernel(tc, X, W, b, class_token, pos_embed, out):
             xp = ahead.tile([128, 8, 128], F32, name="xp")
             dst = xp[:].bitcast(BF16).rearrange("p gx (py px) -> p gx py px", px=16)
             src = xs[i][:].rearrange("p (py gx px) -> p gx py px", py=16, gx=8)
-            nv = 8 if i < 2 else 6
-            nc.vector.tensor_copy(out=dst[:, 0:nv], in_=src[:, 0:nv])
-            if nv < 8:
-                nc.gpsimd.tensor_scalar(out=dst[:, nv:8], in0=src[:, nv:8], scalar1=1.0, scalar2=0.0, op0=MULT, op1=mybir.AluOpType.add)
+            pieces = 2 if i == 0 else 1
+            for r in range(pieces):
+                rows = slice(r * 16 // pieces, (r + 1) * 16 // pieces)
+                nc.vector.tensor_copy(out=dst[:, :, rows], in_=src[:, :, rows])
             st[("xp", i)] = xp
 
         def t_in(i, jb):
@@ -226,21 +230,22 @@ def tile_myvit_t_kernel(tc, X, W, b, class_token, pos_embed, out):
             if on(k - 2):
                 times_pos(k - 2, 1)
             if k == 0:
-                bias_column()
                 regroup(3)
             if on(k) and k < last:
                 add_bias(k, 0)
             if k == last:
                 add_bias_columns(last, 0)
+            if k == -1:
+                regroup_w()
             if on(k + 1):
                 quant(k + 1)
             if k == -1:
-                regroup_w()
                 quantise_w()
+                bias_column()
                 regroup(2)
             if k == 0:
                 regroup(4)
-            if k == 2:
+            if k == 8:
                 class_rows()
             if k == 1:
                 regroup(5)

@@ -24,8 +24,9 @@ def tile_myvit_t_kernel(tc, X, W, b, class_token, pos_embed, out):
         work = ctx.enter_context(tc.tile_pool(name="work", bufs=4))
         ahead = ctx.enter_context(tc.tile_pool(name="ahead", bufs=6))
         outp = ctx.enter_context(tc.tile_pool(name="outp", bufs=ITEMS))
-        ps_tp = ctx.enter_context(tc.psum_pool(name="ps_tp", bufs=3))
+        ps_tp = ctx.enter_context(tc.psum_pool(name="ps_tp", bufs=2))
         ps_mid = ctx.enter_context(tc.psum_pool(name="ps_mid", bufs=2))
+        ps_warm = ctx.enter_context(tc.psum_pool(name="ps_warm", bufs=1))
         ps_fin = ctx.enter_context(tc.psum_pool(name="ps_fin", bufs=3))
         ctx.enter_context(tc.manual_schedule())
 
@@ -78,7 +79,7 @@ def tile_myvit_t_kernel(tc, X, W, b, class_token, pos_embed, out):
                     nc.tensor.transpose(wt[:, hh * 2 + c, :], w32[:, hh, c * 128 : (c + 1) * 128], ident[:])
 
         def regroup_w():
-            nc.vector.tensor_copy(
+            nc.scalar.copy(
                 out=wg[:].bitcast(F32).rearrange("p (hh h c) -> p hh h c", hh=2, c=2),
                 in_=wt[:].rearrange("p (hh c) h -> p hh h c", hh=2),
             )
@@ -105,6 +106,12 @@ def tile_myvit_t_kernel(tc, X, W, b, class_token, pos_embed, out):
             nc.sync.dma_start(out=out[:, 0, :], in_=cls_sb[:])
 
         st = {}
+        warm = ps_warm.tile([128, 128], F32, name="warm")
+
+        def keep_warm():
+            nc.tensor.matmul(out=warm[:], lhsT=ident[:], rhs=ident[:], start=True, stop=True)
+
+        last = ITEMS - 1
 
         def regroup(i):
             xp = ahead.tile([128, 8, 128], F32, name="xp")
@@ -128,7 +135,8 @@ def tile_myvit_t_kernel(tc, X, W, b, class_token, pos_embed, out):
             if jb == 0:
                 st[("gq", i)] = work.tile([128, 2048], BF16, name="gq", align_bytes=64)
             gq32 = st[("gq", i)][:].bitcast(F32)
-            nc.scalar.copy(
+            copy_out = nc.vector.tensor_copy if jb == 1 and i < 2 else nc.scalar.copy
+            copy_out(
                 out=gq32[:, jb * 512 : (jb + 1) * 512].rearrange("p (a gxl nc) -> p a gxl nc", gxl=2, nc=16),
                 in_=st[("tp", i, jb)][:].rearrange("p (gxl jj) (gy nc) -> p (jj gy) gxl nc", gxl=2, nc=16),
             )
@@ -167,37 +175,42 @@ def tile_myvit_t_kernel(tc, X, W, b, class_token, pos_embed, out):
 
         def t_out(i, jb):
             a_sb = st[("a", i)]
-            fin = ps_fin.tile([128, 2, 256], F32, name="fin", tag="fin")
-            for jj in range(2):
-                for hh in range(2):
-                    j = 2 * jb + jj
-                    nc.tensor.transpose(fin[:, jj, hh * 128 : (hh + 1) * 128], a_sb[:, hh, j * 128 : (j + 1) * 128], ident[:])
-            st[("fin", i, jb)] = fin
+            pieces = 2 if (i, jb) == (last, 1) else 1
+            st[("fin", i, jb)] = []
+            for r in range(pieces):
+                slots = 2 // pieces
+                fin = ps_fin.tile([128, slots, 256], F32, name="fin", tag="fin")
+                for s in range(slots):
+                    j = 2 * jb + r * slots + s
+                    for hh in range(2):
+                        nc.tensor.transpose(fin[:, s, hh * 128 : (hh + 1) * 128], a_sb[:, hh, j * 128 : (j + 1) * 128], ident[:])
+                st[("fin", i, jb)].append(fin)
 
         def times_pos(i, jb):
             if jb == 0:
                 st[("osb", i)] = outp.tile([128, 1024], F32, name="osb")
             osb = st[("osb", i)]
-            pieces = 2 if (i, jb) == (ITEMS - 1, 1) else 1
-            for s in range(pieces):
-                slots = slice(s, s + 1) if pieces == 2 else slice(0, 2)
-                c0 = jb * 512 + s * 256
-                c1 = c0 + 512 // pieces
+            fins = st[("fin", i, jb)]
+            width = 512 // len(fins)
+            for r, fin in enumerate(fins):
+                c0 = jb * 512 + r * width
+                c1 = c0 + width
                 nc.vector.tensor_tensor(
                     out=osb[:, c0:c1].rearrange("p (s h) -> p s h", h=256),
-                    in0=st[("fin", i, jb)][:, slots, :],
+                    in0=fin[:],
                     in1=pos_a[:, c0:c1].rearrange("p (s h) -> p s h", h=256),
                     op=MULT,
                 )
-                if i == ITEMS - 1:
+                if i == last:
                     nc.sync.dma_start(out=out_i[i][:, :, c0:c1], in_=osb[:, c0:c1])
-            if i < ITEMS - 1 and jb == 1:
+            if i < last and jb == 1:
                 nc.sync.dma_start(out=out_i[i], in_=osb[:])
 
         def on(i):
             return 0 <= i < ITEMS
 
-        last = ITEMS - 1
+        for r in range(8):
+            keep_warm()
         regroup(0)
         regroup(1)
         for k in range(-1, ITEMS + 2):
@@ -211,6 +224,8 @@ def tile_myvit_t_kernel(tc, X, W, b, class_token, pos_embed, out):
                 t_out(k - 2, 0)
             if k >= 2 and on(k + 4):
                 regroup(k + 4)
+            if k >= 0:
+                keep_warm()
             if on(k + 1):
                 t_in(k + 1, 1)
             if on(k - 2):

@@ -24,10 +24,10 @@ def tile_myvit_t_kernel(tc, X, W, b, class_token, pos_embed, out):
         work = ctx.enter_context(tc.tile_pool(name="work", bufs=4))
         ahead = ctx.enter_context(tc.tile_pool(name="ahead", bufs=6))
         outp = ctx.enter_context(tc.tile_pool(name="outp", bufs=ITEMS))
-        ps_tp = ctx.enter_context(tc.psum_pool(name="ps_tp", bufs=2))
+        ps_tp = ctx.enter_context(tc.psum_pool(name="ps_tp", bufs=3))
         ps_mid = ctx.enter_context(tc.psum_pool(name="ps_mid", bufs=2))
         ps_warm = ctx.enter_context(tc.psum_pool(name="ps_warm", bufs=1))
-        ps_fin = ctx.enter_context(tc.psum_pool(name="ps_fin", bufs=3))
+        ps_fin = ctx.enter_context(tc.psum_pool(name="ps_fin", bufs=2))
         ctx.enter_context(tc.manual_schedule())
 
         zb = const.tile([128, 256], BF16, name="zb")
@@ -106,10 +106,10 @@ def tile_myvit_t_kernel(tc, X, W, b, class_token, pos_embed, out):
             nc.sync.dma_start(out=out[:, 0, :], in_=cls_sb[:])
 
         st = {}
-        warm = ps_warm.tile([128, 128], F32, name="warm")
+        warm = ps_warm.tile([128, 4, 128], F32, name="warm")
 
-        def keep_warm():
-            nc.tensor.matmul(out=warm[:], lhsT=ident[:], rhs=ident[:], start=True, stop=True)
+        def keep_warm(r):
+            nc.tensor.matmul(out=warm[:, r % 4, :], lhsT=ident[:], rhs=ident[:], start=True, stop=True)
 
         last = ITEMS - 1
 
@@ -179,7 +179,10 @@ def tile_myvit_t_kernel(tc, X, W, b, class_token, pos_embed, out):
             st[("fin", i, jb)] = []
             for r in range(pieces):
                 slots = 2 // pieces
-                fin = ps_fin.tile([128, slots, 256], F32, name="fin", tag="fin")
+                if pieces == 2:
+                    fin = ps_tp.tile([128, slots, 256], F32, name="fin", tag="tp")
+                else:
+                    fin = ps_fin.tile([128, slots, 256], F32, name="fin", tag="fin")
                 for s in range(slots):
                     j = 2 * jb + r * slots + s
                     for hh in range(2):
@@ -209,8 +212,8 @@ def tile_myvit_t_kernel(tc, X, W, b, class_token, pos_embed, out):
         def on(i):
             return 0 <= i < ITEMS
 
-        for r in range(8):
-            keep_warm()
+        for r in range(4):
+            keep_warm(r)
         regroup(0)
         regroup(1)
         for k in range(-1, ITEMS + 2):
@@ -225,7 +228,7 @@ def tile_myvit_t_kernel(tc, X, W, b, class_token, pos_embed, out):
             if k >= 2 and on(k + 4):
                 regroup(k + 4)
             if k >= 0:
-                keep_warm()
+                keep_warm(k)
             if on(k + 1):
                 t_in(k + 1, 1)
             if on(k - 2):

@@ -26,8 +26,7 @@ def tile_myvit_t_kernel(tc, X, W, b, class_token, pos_embed, out):
         outp = ctx.enter_context(tc.tile_pool(name="outp", bufs=ITEMS))
         ps_tp = ctx.enter_context(tc.psum_pool(name="ps_tp", bufs=3))
         ps_mid = ctx.enter_context(tc.psum_pool(name="ps_mid", bufs=2))
-        ps_warm = ctx.enter_context(tc.psum_pool(name="ps_warm", bufs=1))
-        ps_fin = ctx.enter_context(tc.psum_pool(name="ps_fin", bufs=2))
+        ps_fin = ctx.enter_context(tc.psum_pool(name="ps_fin", bufs=3))
         ctx.enter_context(tc.manual_schedule())
 
         zb = const.tile([128, 256], BF16, name="zb")
@@ -106,11 +105,6 @@ def tile_myvit_t_kernel(tc, X, W, b, class_token, pos_embed, out):
             nc.sync.dma_start(out=out[:, 0, :], in_=cls_sb[:])
 
         st = {}
-        warm = ps_warm.tile([128, 4, 128], F32, name="warm")
-
-        def keep_warm(r):
-            nc.tensor.matmul(out=warm[:, r % 4, :], lhsT=ident[:], rhs=ident[:], start=True, stop=True)
-
         last = ITEMS - 1
 
         def regroup(i):
@@ -212,8 +206,9 @@ def tile_myvit_t_kernel(tc, X, W, b, class_token, pos_embed, out):
         def on(i):
             return 0 <= i < ITEMS
 
+        warm = ps_tp.tile([128, 4, 128], F32, name="warm", tag="tp")
         for r in range(4):
-            keep_warm(r)
+            nc.tensor.matmul(out=warm[:, r, :], lhsT=ident[:], rhs=ident[:], start=True, stop=True)
         regroup(0)
         regroup(1)
         for k in range(-1, ITEMS + 2):
@@ -227,8 +222,6 @@ def tile_myvit_t_kernel(tc, X, W, b, class_token, pos_embed, out):
                 t_out(k - 2, 0)
             if k >= 2 and on(k + 4):
                 regroup(k + 4)
-            if k >= 0:
-                keep_warm(k)
             if on(k + 1):
                 t_in(k + 1, 1)
             if on(k - 2):

@@ -95,11 +95,16 @@ def tile_myvit_t_kernel(tc, X, W, b, class_token, pos_embed, out):
                 nc.tensor.matmul(out=bc[:, hh, :], lhsT=zb[:, hh * 128 : (hh + 1) * 128], rhs=ones[:, 0:64], start=True, stop=True)
             nc.vector.tensor_copy(out=b_col[:], in_=bc[:, :, 0])
 
-        cls_in = const.tile([128, 2, 256], BF16, name="cls_in")
-        nc.sync.dma_start(out=cls_in[:, 0, :], in_=class_token[0, :].partition_broadcast(128))
-        nc.sync.dma_start(out=cls_in[:, 1, :], in_=pos_embed[0, :].partition_broadcast(128))
+        zc = const.tile([128, 512], BF16, name="zc")
+        nc.gpsimd.memset(zc[:], 0.0)
+        nc.sync.dma_start(out=zc[0:1, 0:256], in_=class_token)
+        nc.sync.dma_start(out=zc[0:1, 256:512], in_=pos_embed[0:1, :])
 
         def class_rows():
+            zp = ps_fin.tile([128, 2, 256], F32, name="zp", tag="fin")
+            nc.tensor.matmul(out=zp[:].rearrange("p t h -> p (t h)"), lhsT=ones[:], rhs=zc[:], start=True, stop=True)
+            cls_in = const.tile([128, 2, 256], F32, name="cls_in")
+            nc.scalar.copy(out=cls_in[:], in_=zp[:])
             cls_sb = const.tile([128, 256], F32, name="cls_sb")
             nc.gpsimd.tensor_tensor(out=cls_sb[:], in0=cls_in[:, 0, :], in1=cls_in[:, 1, :], op=MULT)
             nc.sync.dma_start(out=out[:, 0, :], in_=cls_sb[:])
@@ -220,8 +225,6 @@ def tile_myvit_t_kernel(tc, X, W, b, class_token, pos_embed, out):
                 add_bias_columns(last, 1)
             if on(k - 2):
                 t_out(k - 2, 0)
-            if k >= 2 and on(k + 4):
-                regroup(k + 4)
             if on(k + 1):
                 t_in(k + 1, 1)
             if on(k - 2):
@@ -240,8 +243,6 @@ def tile_myvit_t_kernel(tc, X, W, b, class_token, pos_embed, out):
                 e_in(k + 1, 1)
             if on(k - 2):
                 times_pos(k - 2, 1)
-            if k == 0:
-                regroup(3)
             if on(k) and k < last:
                 add_bias(k, 0)
             if k == last:
@@ -253,10 +254,7 @@ def tile_myvit_t_kernel(tc, X, W, b, class_token, pos_embed, out):
             if k == -1:
                 quantise_w()
                 bias_column()
-                regroup(2)
-            if k == 0:
-                regroup(4)
+            if k >= -1 and on(k + 3):
+                regroup(k + 3)
             if k == 8:
                 class_rows()
-            if k == 1:
-                regroup(5)

from contextlib import ExitStack

import concourse.mybir as mybir
from concourse.masks import make_identity

BF16 = mybir.dt.bfloat16
F32 = mybir.dt.float32
U32 = mybir.dt.uint32
U8 = mybir.dt.uint8
FP8X4 = mybir.dt.float8_e4m3fn_x4
MULT = mybir.AluOpType.mult
IDENT = mybir.ActivationFunctionType.Identity

FLOPS = 2 * 8192 * 512 * 256

ITEMS = 16


def tile_myvit_t_kernel(tc, X, W, b, class_token, pos_embed, out):
    nc = tc.nc
    with ExitStack() as ctx:
        const = ctx.enter_context(tc.tile_pool(name="const", bufs=1))
        xin = ctx.enter_context(tc.tile_pool(name="xin", bufs=1))
        work = ctx.enter_context(tc.tile_pool(name="work", bufs=4))
        ahead = ctx.enter_context(tc.tile_pool(name="ahead", bufs=6))
        outp = ctx.enter_context(tc.tile_pool(name="outp", bufs=ITEMS))
        ps_tp = ctx.enter_context(tc.psum_pool(name="ps_tp", bufs=3))
        ps_mid = ctx.enter_context(tc.psum_pool(name="ps_mid", bufs=2))
        ps_fin = ctx.enter_context(tc.psum_pool(name="ps_fin", bufs=3))
        ctx.enter_context(tc.manual_schedule())

        zb = const.tile([128, 256], BF16, name="zb")
        nc.vector.memset(zb[:], 0.0)
        ones = const.tile([128, 128], BF16, name="ones")
        nc.vector.memset(ones[:], 1.0)
        ident = const.tile([128, 128], F32, name="ident")
        make_identity(nc, ident[:])

        w_sb = const.tile([128, 2, 512], BF16, name="w_sb")
        xrows = X.rearrange("n c (gy py) x -> (n c gy) (py x)", gy=8)
        xs = []

        def load_item(i):
            xt = xin.tile([128, 2048], BF16, name="xs%d" % i)
            pieces = 2 if i == 0 else 1
            for r in range(pieces):
                cols = slice(r * 2048 // pieces, (r + 1) * 2048 // pieces)
                nc.sync.dma_start(out=xt[:, cols], in_=xrows[i * 128 : (i + 1) * 128, cols])
            xs.append(xt)

        load_item(0)
        load_item(1)
        nc.sync.dma_start(out=w_sb[:], in_=W.rearrange("(hh h) k -> h hh k", hh=2))
        nc.sync.dma_start(out=zb[0:1, :], in_=b.unsqueeze(0))
        load_item(2)
        pos_a = const.tile([128, 1024], BF16, name="pos_a")
        pos_rows = pos_embed[1:65, :].rearrange("(q j) h -> q (j h)", j=4)
        nc.sync.dma_start(out=pos_a[:], in_=pos_rows.unsqueeze(1).to_broadcast([16, 8, 1024]))
        for i in range(3, ITEMS):
            load_item(i)

        perm = const.tile([128, 128], F32, name="perm")
        nc.vector.tensor_copy(
            out=perm[:].rearrange("p (gy nc) -> p gy nc", gy=8),
            in_=ident[:].rearrange("p (nc gy) -> p gy nc", gy=8),
        )

        wg = const.tile([128, 1024], BF16, name="wg", align_bytes=64)
        wcodes = const.tile([128, 256], U32, name="wcodes", align_bytes=64)
        wscl = const.tile([128, 256], U8, name="wscl", align_bytes=64)

        wt = ps_fin.tile([128, 4, 128], F32, name="wt", tag="fin")

        def transpose_w():
            w32 = w_sb[:].bitcast(F32)
            for hh in range(2):
                for c in range(2):
                    nc.tensor.transpose(wt[:, hh * 2 + c, :], w32[:, hh, c * 128 : (c + 1) * 128], ident[:])

        def regroup_w():
            nc.scalar.copy(
                out=wg[:].bitcast(F32).rearrange("p (hh h c) -> p hh h c", hh=2, c=2),
                in_=wt[:].rearrange("p (hh c) h -> p hh h c", hh=2),
            )

        def quantise_w():
            nc.vector.quantize_mx(out=wcodes[:].bitcast(FP8X4), scales=wscl[:], in_=wg[:])

        out_i = out[:, 1:65, :].rearrange("(i n) (q j) h -> i q n (j h)", n=8, j=4)
        b_col = const.tile([128, 2], F32, name="b_col")

        def bias_column():
            bc = ps_fin.tile([128, 2, 64], F32, name="bc", tag="fin")
            for hh in range(2):
                nc.tensor.matmul(out=bc[:, hh, :], lhsT=zb[:, hh * 128 : (hh + 1) * 128], rhs=ones[:, 0:64], start=True, stop=True)
            nc.vector.tensor_copy(out=b_col[:], in_=bc[:, :, 0])

        zc = const.tile([128, 512], BF16, name="zc")
        nc.gpsimd.memset(zc[:], 0.0)
        nc.sync.dma_start(out=zc[0:1, 0:256], in_=class_token)
        nc.sync.dma_start(out=zc[0:1, 256:512], in_=pos_embed[0:1, :])

        def class_rows():
            zp = ps_fin.tile([128, 2, 256], F32, name="zp", tag="fin")
            nc.tensor.matmul(out=zp[:].rearrange("p t h -> p (t h)"), lhsT=ones[:], rhs=zc[:], start=True, stop=True)
            cls_in = const.tile([128, 2, 256], F32, name="cls_in")
            nc.scalar.copy(out=cls_in[:], in_=zp[:])
            cls_sb = const.tile([128, 256], F32, name="cls_sb")
            nc.gpsimd.tensor_tensor(out=cls_sb[:], in0=cls_in[:, 0, :], in1=cls_in[:, 1, :], op=MULT)
            nc.sync.dma_start(out=out[:, 0, :], in_=cls_sb[:])

        st = {}
        last = ITEMS - 1

        def regroup(i):
            xp = ahead.tile([128, 8, 128], F32, name="xp")
            dst = xp[:].bitcast(BF16).rearrange("p gx (py px) -> p gx py px", px=16)
            src = xs[i][:].rearrange("p (py gx px) -> p gx py px", py=16, gx=8)
            pieces = 2 if i == 0 else 1
            for r in range(pieces):
                rows = slice(r * 16 // pieces, (r + 1) * 16 // pieces)
                nc.vector.tensor_copy(out=dst[:, :, rows], in_=src[:, :, rows])
            st[("xp", i)] = xp

        def t_in(i, jb):
            xp = st[("xp", i)]
            tp = ps_tp.tile([128, 4, 128], F32, name="tp", tag="tp")
            for s in range(4):
                gxl, jj = s // 2, s % 2
                nc.tensor.transpose(tp[:, s, :], xp[:, 4 * gxl + 2 * jb + jj, :], perm[:])
            st[("tp", i, jb)] = tp

        def e_in(i, jb):
            if jb == 0:
                st[("gq", i)] = work.tile([128, 2048], BF16, name="gq", align_bytes=64)
            gq32 = st[("gq", i)][:].bitcast(F32)
            copy_out = nc.vector.tensor_copy if jb == 1 and i < 2 else nc.scalar.copy
            copy_out(
                out=gq32[:, jb * 512 : (jb + 1) * 512].rearrange("p (a gxl nc) -> p a gxl nc", gxl=2, nc=16),
                in_=st[("tp", i, jb)][:].rearrange("p (gxl jj) (gy nc) -> p (jj gy) gxl nc", gxl=2, nc=16),
            )

        def quant(i):
            codes = work.tile([128, 512], U32, name="codes", align_bytes=64)
            scl = work.tile([128, 512], U8, name="scl", align_bytes=64)
            nc.vector.quantize_mx(out=codes[:].bitcast(FP8X4), scales=scl[:], in_=st[("gq", i)][:])
            st[("codes", i)] = codes
            st[("scl", i)] = scl

        def mx(i, hh):
            mid = ps_mid.tile([128, 512], F32, name="mid", tag="mid")
            nc.tensor.matmul_mx(
                out=mid[:],
                lhsT=wcodes[:, hh * 128 : (hh + 1) * 128].bitcast(FP8X4),
                lhsT_scale=wscl[:, hh * 128 : (hh + 1) * 128],
                rhs=st[("codes", i)][:].bitcast(FP8X4),
                rhs_scale=st[("scl", i)][:],
                start=True,
                stop=True,
            )
            st[("mid", i, hh)] = mid

        def add_bias(i, hh):
            if hh == 0:
                st[("a", i)] = work.tile([128, 2, 512], F32, name="a_sb")
            nc.scalar.activation(out=st[("a", i)][:, hh, :], in_=st[("mid", i, hh)][:], func=IDENT, bias=b_col[:, hh : hh + 1], scale=1.0)

        def add_bias_columns(i, jb):
            if jb == 0:
                st[("a", i)] = work.tile([128, 2, 512], F32, name="a_sb")
            cols = slice(jb * 256, (jb + 1) * 256)
            for hh in range(2):
                nc.scalar.activation(out=st[("a", i)][:, hh, cols], in_=st[("mid", i, hh)][:, cols], func=IDENT, bias=b_col[:, hh : hh + 1], scale=1.0)

        def t_out(i, jb):
            a_sb = st[("a", i)]
            pieces = 2 if (i, jb) == (last, 1) else 1
            st[("fin", i, jb)] = []
            for r in range(pieces):
                slots = 2 // pieces
                if pieces == 2:
                    fin = ps_tp.tile([128, slots, 256], F32, name="fin", tag="tp")
                else:
                    fin = ps_fin.tile([128, slots, 256], F32, name="fin", tag="fin")
                for s in range(slots):
                    j = 2 * jb + r * slots + s
                    for hh in range(2):
                        nc.tensor.transpose(fin[:, s, hh * 128 : (hh + 1) * 128], a_sb[:, hh, j * 128 : (j + 1) * 128], ident[:])
                st[("fin", i, jb)].append(fin)

        def times_pos(i, jb):
            if jb == 0:
                st[("osb", i)] = outp.tile([128, 1024], F32, name="osb")
            osb = st[("osb", i)]
            fins = st[("fin", i, jb)]
            width = 512 // len(fins)
            for r, fin in enumerate(fins):
                c0 = jb * 512 + r * width
                c1 = c0 + width
                nc.vector.tensor_tensor(
                    out=osb[:, c0:c1].rearrange("p (s h) -> p s h", h=256),
                    in0=fin[:],
                    in1=pos_a[:, c0:c1].rearrange("p (s h) -> p s h", h=256),
                    op=MULT,
                )
                if i == last:
                    nc.sync.dma_start(out=out_i[i][:, :, c0:c1], in_=osb[:, c0:c1])
            if i < last and jb == 1:
                nc.sync.dma_start(out=out_i[i], in_=osb[:])

        def on(i):
            return 0 <= i < ITEMS

        warm = ps_tp.tile([128, 4, 128], F32, name="warm", tag="tp")
        for r in range(4):
            nc.tensor.matmul(out=warm[:, r, :], lhsT=ident[:], rhs=ident[:], start=True, stop=True)
        regroup(0)
        regroup(1)
        for k in range(-1, ITEMS + 2):
            if on(k + 1):
                t_in(k + 1, 0)
            if on(k - 1) and k - 1 < last:
                add_bias(k - 1, 1)
            if k - 1 == last:
                add_bias_columns(last, 1)
            if on(k - 2):
                t_out(k - 2, 0)
            if on(k + 1):
                t_in(k + 1, 1)
            if on(k - 2):
                t_out(k - 2, 1)
            if k == -1:
                transpose_w()
            if on(k + 1):
                e_in(k + 1, 0)
            if on(k):
                mx(k, 0)
            if on(k - 2):
                times_pos(k - 2, 0)
            if on(k):
                mx(k, 1)
            if on(k + 1):
                e_in(k + 1, 1)
            if on(k - 2):
                times_pos(k - 2, 1)
            if on(k) and k < last:
                add_bias(k, 0)
            if k == last:
                add_bias_columns(last, 0)
            if k == -1:
                regroup_w()
            if on(k + 1):
                quant(k + 1)
            if k == -1:
                quantise_w()
                bias_column()
            if k >= -1 and on(k + 3):
                regroup(k + 3)
            if k == 8:
                class_rows()
